import numpy as np
import ml_dtypes


def mxq(x, axis, fmt="e4m3"):
    dtype, down = {"e4m3": (ml_dtypes.float8_e4m3fn, 7), "e5m2": (ml_dtypes.float8_e5m2, 14)}[fmt]
    v = np.moveaxis(np.asarray(x, np.float32).astype(ml_dtypes.bfloat16).astype(np.float64), axis, -1)
    blocks = v.reshape(v.shape[:-1] + (-1, 32))
    amax = np.abs(blocks).max(-1, keepdims=True)
    byte = np.maximum(np.where(amax > 0, np.frexp(amax)[1] - 1 + 127, 0) - down, 1)
    scale = np.exp2(byte - 127.0)
    codes = (blocks / scale).astype(np.float32).astype(dtype).astype(np.float64)
    return np.moveaxis((codes * scale).reshape(v.shape), -1, axis)


WIDE = False


def mx_kscale(k):
    if not WIDE:
        return np.ones(k)
    levels = np.array([10, -10, 5, -5, 0])
    if k % 512:
        return np.exp2(np.random.permutation(np.resize(levels, k // 32))).repeat(32)
    a = np.empty((k // 512, 16))
    for p in range(k // 512):
        a[p, :8] = np.random.permutation(np.resize(levels, 8))
        for g in range(8):
            far = levels[np.abs(levels - a[p, g]) >= 10]
            a[p, g + 8] = far[np.random.randint(len(far))]
    return np.exp2(a.ravel()).repeat(32)


BF16 = ml_dtypes.bfloat16


def bf(x):
    return np.asarray(x, np.float32).astype(BF16)


def f64(x):
    return np.asarray(x).astype(np.float64)


E2M1 = np.array([0.0, 0.5, 1.0, 1.5, 2.0, 3.0, 4.0, 6.0, -0.0, -0.5, -1.0, -1.5, -2.0, -3.0, -4.0, -6.0])


def pack_weight(w, fmt):
    k, n = w.shape
    w = f64(bf(w)).reshape(k // 32, 32, n)
    amax = np.abs(w).max(1)
    if fmt == "e4m3":
        byte = np.frexp(amax)[1] - 1 + 127 - 7
    else:
        mant, ex = np.frexp(amax / 6.0)
        byte = np.where(mant > 0.5, ex, ex - 1) + 127
    byte = np.clip(np.where(amax > 0, byte, 1), 1, 254)
    scaled = (w * np.exp2(127.0 - byte)[:, None, :]).reshape(k, n).astype(np.float32)
    by_word = np.ascontiguousarray(scaled.reshape(k // 512, 128, 4, n).transpose(0, 1, 3, 2))
    if fmt == "e4m3":
        words = by_word.astype(ml_dtypes.float8_e4m3fn).view(np.uint8)
    else:
        c = by_word.astype(ml_dtypes.float4_e2m1fn).view(np.uint8) & 0xF
        words = c[..., 0::2] | (c[..., 1::2] << 4)
    return np.ascontiguousarray(words), np.ascontiguousarray(byte.astype(np.uint8).reshape(k // 512, 16, n))


def unpack_weight(words, scales, fmt):
    g, p, n, _ = words.shape
    if fmt == "e4m3":
        vals = np.ascontiguousarray(words).view(ml_dtypes.float8_e4m3fn).astype(np.float64)
    else:
        nib = np.empty((g, p, n, 4), np.uint8)
        nib[..., 0::2] = words & 0xF
        nib[..., 1::2] = words >> 4
        vals = E2M1[nib]
    vals = vals * np.repeat(np.exp2(scales.astype(np.float64) - 127.0), 8, axis=1)[..., None]
    return vals.transpose(0, 1, 3, 2).reshape(g * 512, n)
def pack4(w):
    words, scales = pack_weight(w, "e2m1")
    return words.reshape(words.shape[0], 128, -1), scales


def unpack4(words, scales):
    return unpack_weight(words.reshape(words.shape[0], 128, -1, 2), scales, "e2m1")


NU, NI, D = 1024, 1024, 512
N = NU + NI


def draw0():
    s, t = mx_kscale(N), mx_kscale(D)
    A = bf(np.random.uniform(0.0, 2.0 / np.sqrt(N), (N, N)) * s)
    features = bf(np.random.standard_normal((N, D)) / s[:, None] * t)
    Wg_words, Wg_scales = pack4(np.random.standard_normal((D, D)) / np.sqrt(D) / t[:, None])
    return {"A": A,
            "features": features,
            "Wg_words": Wg_words,
            "Wg_scales": Wg_scales,
            "bg": bf(np.random.standard_normal(D) * 0.1)}


def core(A, features, Wg_words, Wg_scales, bg):
    agg = mxq(f64(A), 1, "e4m3") @ mxq(f64(features), 0, "e4m3")
    return np.maximum((mxq(agg, 1, "e4m3") @ unpack4(Wg_words, Wg_scales)) + f64(bg), 0.0)


def e4m3fn_bytes(y):
    return np.clip(np.asarray(y, np.float64), -448.0, 448.0).astype(np.float32).astype(ml_dtypes.float8_e4m3fn).view(np.uint8)


def e4m3fn_values(b):
    return np.asarray(b, np.uint8).view(ml_dtypes.float8_e4m3fn).astype(np.float64)


def setup_inputs():
    d = draw0()
    x0 = np.asarray(d['A']).astype(np.float64)
    s = (np.max(np.abs(x0), axis=(0,), keepdims=True) / 448.0).astype(np.float32)
    out = {}
    for k, v in d.items():
        if k == 'A':
            out['A_bytes'] = e4m3fn_bytes(x0 / s.astype(np.float64))
            out['A_scale'] = s
        else:
            out[k] = v
    return out


def reference(A_bytes, A_scale, features, Wg_words, Wg_scales, bg):
    return core(e4m3fn_values(A_bytes) * A_scale.astype(np.float64), features, Wg_words, Wg_scales, bg)

@@ -1,0 +1,259 @@
+from contextlib import ExitStack
+
+import concourse.mybir as mybir
+from concourse.masks import make_identity
+
+F32 = mybir.dt.float32
+BF16 = mybir.dt.bfloat16
+U32 = mybir.dt.uint32
+I32 = mybir.dt.int32
+U8 = mybir.dt.uint8
+FP8 = mybir.dt.float8_e4m3fn
+FP8X4 = mybir.dt.float8_e4m3fn_x4
+FP4X4 = mybir.dt.float4_e2m1fn_x4
+ALU = mybir.AluOpType
+
+NODES = 2048
+D = 512
+P = 128
+PASSES = NODES // 512
+TILES = NODES // P
+FLOPS = 2 * NODES * NODES * D + 2 * NODES * D * D
+F32_MAX = 3.4028234663852886e38
+
+
+def tile_net_pa_w4_kernel(tc, A_bytes, A_scale, features, Wg_words, Wg_scales, bg, out):
+    nc = tc.nc
+    with ExitStack() as ctx:
+        keep = ctx.enter_context(tc.tile_pool(name="keep", bufs=1))
+        flow = ctx.enter_context(tc.tile_pool(name="flow", bufs=3))
+        psum = ctx.enter_context(tc.psum_pool(name="psum", bufs=2))
+        ctx.enter_context(tc.manual_schedule())
+
+        codes_in = [keep.tile([P, NODES], U8, name="abytes%d" % r, align_bytes=64) for r in range(TILES)]
+        scale = keep.tile([P, PASSES, 4], F32, name="scale")
+        f_raw = [keep.tile([P, 4, D], BF16, name="fraw%d" % g, align_bytes=64) for g in range(PASSES)]
+        f_grp = [keep.tile([P, 4, P, 4], BF16, name="fgrp%d" % g, align_bytes=64) for g in range(PASSES)]
+        f_codes = [keep.tile([P, D], U32, name="fcodes%d" % g, align_bytes=64) for g in range(PASSES)]
+        f_scales = [keep.tile([P, D], U8, name="fscales%d" % g, align_bytes=64) for g in range(PASSES)]
+        w_words = keep.tile([P, 2 * D], U8, name="wwords", align_bytes=64)
+        w_scales = keep.tile([P, D], U8, name="wscales", align_bytes=64)
+        bias = keep.tile([P, D], BF16, name="bias", align_bytes=64)
+        ident = keep.tile([P, P], F32, name="ident", align_bytes=64)
+        dummy = keep.tile([P, 1], F32, name="dummy")
+        dummy2 = keep.tile([P, 1], F32, name="dummy2")
+
+        def load_a(r):
+            nc.sync.dma_start(out=codes_in[r][:], in_=A_bytes[r * P : (r + 1) * P, :])
+
+        def load_f(g):
+            nc.sync.dma_start(out=f_raw[g][:], in_=features.rearrange("(g p j) c -> g p j c", p=P, j=4)[g])
+
+        nc.vector.memset(dummy[:], 0.0)
+        nc.scalar.copy(out=dummy2[:], in_=dummy[:])
+        nc.vector.memset(w_scales[:].bitcast(I32), 0)
+        make_identity(nc, ident[:])
+
+        load_a(0)
+        nc.sync.dma_start(out=scale[:], in_=A_scale.rearrange("o (g p t) -> p (o g) t", p=P, t=4))
+        load_f(0)
+        load_f(1)
+        load_a(1)
+        load_f(2)
+        load_f(3)
+        load_a(2)
+        nc.sync.dma_start(out=w_words[:], in_=Wg_words.rearrange("g p w -> p (g w)"))
+        for q in range(4):
+            nc.sync.dma_start(
+                out=w_scales[32 * q : 32 * q + 4, :].bitcast(I32),
+                in_=Wg_scales.rearrange("g q n -> (g q) n")[4 * q : 4 * q + 4, :].bitcast(I32),
+            )
+        nc.sync.dma_start(out=bias[:], in_=bg.partition_broadcast(P))
+        for r in range(3, TILES):
+            load_a(r)
+
+        wide = {}
+        banks = {}
+        grouped = {}
+        a_codes = {}
+        a_scales = {}
+        acc = {}
+        g_bf = {}
+        g_codes = {}
+        g_scales = {}
+        res = {}
+
+        def cast(r, half, vector=False):
+            if half == 0:
+                wide[r] = flow.tile([P, NODES], BF16, name="wide", align_bytes=64)
+            cols = slice(half * 1024, (half + 1) * 1024)
+            src = codes_in[r][:, cols].bitcast(FP8)
+            if vector:
+                nc.vector.tensor_copy(out=wide[r][:, cols], in_=src)
+            else:
+                nc.scalar.copy(out=wide[r][:, cols], in_=src)
+
+        def turn(r):
+            words = wide[r][:].bitcast(F32)
+            for b in range(2):
+                bank = psum.tile([P, 2, 2, P], F32, name="turn%d" % b)
+                banks[r, b] = bank
+                for gl in range(2):
+                    for u in range(2):
+                        w0 = 256 * (2 * b + gl)
+                        nc.tensor.transpose(bank[:, u, gl, :], words[:, w0 + u : w0 + 256 : 2], ident[:])
+
+        def product(r, b):
+            if b == 0:
+                grouped[r] = flow.tile([P, PASSES, P, 4], BF16, name="grouped", align_bytes=64)
+            in0 = banks[r, b][:].bitcast(BF16).rearrange("p u g (i e) -> p g i u e", e=2)
+            in1 = scale[:, 2 * b : 2 * b + 2, :].rearrange("p g (u e) -> p g u e", e=2)
+            in1 = in1.unsqueeze(2).to_broadcast([P, 2, P, 2, 2])
+            dst = grouped[r][:, 2 * b : 2 * b + 2].rearrange("p g i (u e) -> p g i u e", e=2)
+            nc.vector.tensor_tensor(out=dst, in0=in0, in1=in1, op=ALU.mult)
+
+        def quant_a(r):
+            a_codes[r] = flow.tile([P, PASSES, P], U32, name="acodes", align_bytes=64)
+            a_scales[r] = flow.tile([P, PASSES, P], U8, name="ascales", align_bytes=64)
+            nc.vector.quantize_mx(
+                out=a_codes[r][:].rearrange("p g i -> p (g i)").bitcast(FP8X4),
+                scales=a_scales[r][:].rearrange("p g i -> p (g i)"),
+                in_=grouped[r][:].rearrange("p g i t -> p (g i t)"),
+            )
+
+        def first_matmul(r):
+            acc[r] = psum.tile([P, 4, P], F32, name="acc")
+            for t in range(4):
+                for g in range(PASSES):
+                    nc.tensor.matmul_mx(
+                        out=acc[r][:, t, :],
+                        lhsT=f_codes[g][:, t * P : (t + 1) * P].bitcast(FP8X4),
+                        lhsT_scale=f_scales[g][:, t * P : (t + 1) * P],
+                        rhs=a_codes[r][:, g, :].bitcast(FP8X4),
+                        rhs_scale=a_scales[r][:, g, :],
+                        start=(g == 0),
+                        stop=(g == PASSES - 1),
+                    )
+
+        def agg_out(r):
+            g_bf[r] = flow.tile([P, P, 4], BF16, name="gbf", align_bytes=64)
+            nc.scalar.copy(out=g_bf[r][:], in_=acc[r][:].rearrange("p t i -> p i t"))
+
+        def quant_agg(r):
+            g_codes[r] = flow.tile([P, P], U32, name="gcodes", align_bytes=64)
+            g_scales[r] = flow.tile([P, P], U8, name="gscales", align_bytes=64)
+            nc.vector.quantize_mx(
+                out=g_codes[r][:].bitcast(FP8X4),
+                scales=g_scales[r][:],
+                in_=g_bf[r][:].rearrange("p i t -> p (i t)"),
+            )
+
+        def second_matmul(r):
+            res[r] = psum.tile([P, D], F32, name="res")
+            nc.tensor.matmul_mx(
+                out=res[r][:],
+                lhsT=g_codes[r][:].bitcast(FP8X4),
+                lhsT_scale=g_scales[r][:],
+                rhs=w_words[:].bitcast(FP4X4),
+                rhs_scale=w_scales[:],
+                start=True,
+                stop=True,
+            )
+
+        raw = {}
+        fin = {}
+        mids = {}
+
+        def res_out(r):
+            raw[r] = flow.tile([P, D], F32, name="rawout", align_bytes=64)
+            nc.scalar.copy(out=raw[r][:], in_=res[r][:])
+
+        def finish_gp(r):
+            mid = flow.tile([P, D], F32, name="mid", align_bytes=64)
+            fin[r] = flow.tile([P, D], F32, name="fin", align_bytes=64)
+            nc.gpsimd.tensor_tensor(out=mid[:], in0=raw[r][:], in1=bias[:], op=ALU.add)
+            mids[r] = mid
+
+        def relu(r):
+            nc.scalar.activation(out=fin[r][:], in_=mids[r][:], func=mybir.ActivationFunctionType.Relu)
+            store(r)
+
+        def finish_fast(r):
+            mid = flow.tile([P, D], F32, name="rawout", align_bytes=64)
+            fin[r] = flow.tile([P, D], F32, name="fin", align_bytes=64)
+            for h in range(2):
+                cols = slice(h * 256, (h + 1) * 256)
+                nc.vector.tensor_tensor(out=mid[:, cols], in0=res[r][:, cols], in1=bias[:, cols], op=ALU.add)
+                nc.scalar.activation(out=fin[r][:, cols], in_=mid[:, cols], func=mybir.ActivationFunctionType.Relu)
+            store(r)
+
+        def store(r):
+            nc.sync.dma_start(out=out[r * P : (r + 1) * P, :], in_=fin[r][:])
+
+        def f_interleave(g, engine):
+            src = f_raw[g][:].rearrange("p j (m t) -> p t m j", t=4)
+            if engine == "v":
+                nc.vector.tensor_copy(out=f_grp[g][:], in_=src)
+            elif engine == "s":
+                nc.scalar.copy(out=f_grp[g][:], in_=src)
+            else:
+                nc.gpsimd.tensor_scalar(out=f_grp[g][:], in0=src, scalar1=1.0, scalar2=0.0, op0=ALU.mult, op1=ALU.add)
+
+        def f_quant(g):
+            nc.vector.quantize_mx(
+                out=f_codes[g][:].bitcast(FP8X4),
+                scales=f_scales[g][:],
+                in_=f_grp[g][:].rearrange("p t m j -> p (t m j)"),
+            )
+
+        cast(0, 0, vector=True)
+        cast(0, 1)
+        f_interleave(0, "v")
+        f_interleave(1, "g")
+        turn(0)
+        cast(1, 0)
+        cast(1, 1)
+        f_interleave(2, "s")
+        f_interleave(3, "g")
+
+        def within(r, hi=TILES):
+            return 0 <= r < hi
+
+        FAST = TILES - 2
+        for s in range(TILES + 5):
+            if within(s):
+                product(s, 0)
+            if s == 0:
+                f_quant(0)
+            if s == 1:
+                f_quant(2)
+            if within(s + 2):
+                cast(s + 2, 0)
+            if within(s + 1):
+                turn(s + 1)
+            if within(s - 2):
+                agg_out(s - 2)
+            if within(s - 3):
+                second_matmul(s - 3)
+            if within(s - 1):
+                quant_a(s - 1)
+            if within(s):
+                product(s, 1)
+            if s == 0:
+                f_quant(1)
+            if s == 1:
+                f_quant(3)
+            if FAST <= s - 3 < TILES:
+                finish_fast(s - 3)
+            if within(s - 2):
+                quant_agg(s - 2)
+            if within(s - 1):
+                first_matmul(s - 1)
+            if within(s - 3, FAST):
+                res_out(s - 3)
+            if within(s + 2):
+                cast(s + 2, 1)
+            if within(s - 4, FAST):
+                relu(s - 4)
+            if within(s - 3, FAST):
+                finish_gp(s - 3)

@@ -12,6 +12,7 @@ FP8 = mybir.dt.float8_e4m3fn
 FP8X4 = mybir.dt.float8_e4m3fn_x4
 FP4X4 = mybir.dt.float4_e2m1fn_x4
 ALU = mybir.AluOpType
+ACT = mybir.ActivationFunctionType
 
 NODES = 2048
 D = 512
@@ -19,7 +20,6 @@ P = 128
 PASSES = NODES // 512
 TILES = NODES // P
 FLOPS = 2 * NODES * NODES * D + 2 * NODES * D * D
-F32_MAX = 3.4028234663852886e38
 
 
 def tile_net_pa_w4_kernel(tc, A_bytes, A_scale, features, Wg_words, Wg_scales, bg, out):
@@ -27,11 +27,12 @@ def tile_net_pa_w4_kernel(tc, A_bytes, A_scale, features, Wg_words, Wg_scales, b
     with ExitStack() as ctx:
         keep = ctx.enter_context(tc.tile_pool(name="keep", bufs=1))
         flow = ctx.enter_context(tc.tile_pool(name="flow", bufs=3))
-        psum = ctx.enter_context(tc.psum_pool(name="psum", bufs=2))
+        psum = ctx.enter_context(tc.psum_pool(name="psum", bufs=1))
         ctx.enter_context(tc.manual_schedule())
 
         codes_in = [keep.tile([P, NODES], U8, name="abytes%d" % r, align_bytes=64) for r in range(TILES)]
         scale = keep.tile([P, PASSES, 4], F32, name="scale")
+        spread = [keep.tile([P, NODES // 2], F32, name="spread%d" % h, align_bytes=64) for h in range(2)]
         f_raw = [keep.tile([P, 4, D], BF16, name="fraw%d" % g, align_bytes=64) for g in range(PASSES)]
         f_grp = [keep.tile([P, 4, P, 4], BF16, name="fgrp%d" % g, align_bytes=64) for g in range(PASSES)]
         f_codes = [keep.tile([P, D], U32, name="fcodes%d" % g, align_bytes=64) for g in range(PASSES)]
@@ -39,7 +40,9 @@ def tile_net_pa_w4_kernel(tc, A_bytes, A_scale, features, Wg_words, Wg_scales, b
         w_words = keep.tile([P, 2 * D], U8, name="wwords", align_bytes=64)
         w_scales = keep.tile([P, D], U8, name="wscales", align_bytes=64)
         bias = keep.tile([P, D], BF16, name="bias", align_bytes=64)
+        bias_col = keep.tile([P, 4], F32, name="biascol")
         ident = keep.tile([P, P], F32, name="ident", align_bytes=64)
+        ident_bf = keep.tile([P, P], BF16, name="identbf", align_bytes=64)
         dummy = keep.tile([P, 1], F32, name="dummy")
         dummy2 = keep.tile([P, 1], F32, name="dummy2")
 
@@ -49,28 +52,52 @@ def tile_net_pa_w4_kernel(tc, A_bytes, A_scale, features, Wg_words, Wg_scales, b
         def load_f(g):
             nc.sync.dma_start(out=f_raw[g][:], in_=features.rearrange("(g p j) c -> g p j c", p=P, j=4)[g])
 
+        def load_spread(h):
+            row = A_scale.rearrange("o k -> (o k)")[h * 1024 : (h + 1) * 1024]
+            nc.sync.dma_start(out=spread[h][:], in_=row.partition_broadcast(P))
+
+        def load_w():
+            nc.sync.dma_start(out=w_words[:], in_=Wg_words.rearrange("g p w -> p (g w)"))
+            for q in range(4):
+                nc.sync.dma_start(
+                    out=w_scales[32 * q : 32 * q + 4, :].bitcast(I32),
+                    in_=Wg_scales.rearrange("g q n -> (g q) n")[4 * q : 4 * q + 4, :].bitcast(I32),
+                )
+            nc.sync.dma_start(out=bias[:], in_=bg.partition_broadcast(P))
+
         nc.vector.memset(dummy[:], 0.0)
         nc.scalar.copy(out=dummy2[:], in_=dummy[:])
         nc.vector.memset(w_scales[:].bitcast(I32), 0)
         make_identity(nc, ident[:])
+        nc.vector.tensor_copy(out=ident_bf[:], in_=ident[:])
+
+        def load_scale():
+            nc.sync.dma_start(out=scale[:], in_=A_scale.rearrange("o (g p t) -> p (o g) t", p=P, t=4))
 
         load_a(0)
-        nc.sync.dma_start(out=scale[:], in_=A_scale.rearrange("o (g p t) -> p (o g) t", p=P, t=4))
+        load_scale()
         load_f(0)
         load_f(1)
         load_a(1)
+        load_spread(0)
+        load_spread(1)
         load_f(2)
         load_f(3)
         load_a(2)
-        nc.sync.dma_start(out=w_words[:], in_=Wg_words.rearrange("g p w -> p (g w)"))
-        for q in range(4):
-            nc.sync.dma_start(
-                out=w_scales[32 * q : 32 * q + 4, :].bitcast(I32),
-                in_=Wg_scales.rearrange("g q n -> (g q) n")[4 * q : 4 * q + 4, :].bitcast(I32),
-            )
-        nc.sync.dma_start(out=bias[:], in_=bg.partition_broadcast(P))
-        for r in range(3, TILES):
-            load_a(r)
+        load_w()
+        load_a(3)
+        load_a(4)
+        load_a(5)
+        load_a(6)
+        load_a(7)
+        load_a(8)
+        load_a(9)
+        load_a(10)
+        load_a(11)
+        load_a(12)
+        load_a(13)
+        load_a(14)
+        load_a(15)
 
         wide = {}
         banks = {}
@@ -81,40 +108,59 @@ def tile_net_pa_w4_kernel(tc, A_bytes, A_scale, features, Wg_words, Wg_scales, b
         g_bf = {}
         g_codes = {}
         g_scales = {}
-        res = {}
+        mid = {}
+        t1 = {}
+        t2 = {}
 
-        def cast(r, half, vector=False):
-            if half == 0:
-                wide[r] = flow.tile([P, NODES], BF16, name="wide", align_bytes=64)
+        def cast(r, half, engine):
+            if r not in wide:
+                wide[r] = flow.tile([P, NODES], BF16, name="wide", bufs=5, align_bytes=64)
             cols = slice(half * 1024, (half + 1) * 1024)
             src = codes_in[r][:, cols].bitcast(FP8)
-            if vector:
+            if engine == "v":
                 nc.vector.tensor_copy(out=wide[r][:, cols], in_=src)
             else:
                 nc.scalar.copy(out=wide[r][:, cols], in_=src)
 
-        def turn(r):
+        def scaled(r, half):
+            if r not in wide:
+                wide[r] = flow.tile([P, NODES], BF16, name="wide", bufs=5, align_bytes=64)
+            cols = slice(half * 1024, (half + 1) * 1024)
+            nc.vector.tensor_tensor(
+                out=wide[r][:, cols], in0=codes_in[r][:, cols].bitcast(FP8), in1=spread[half][:], op=ALU.mult
+            )
+
+        def turn(r, b):
             words = wide[r][:].bitcast(F32)
-            for b in range(2):
-                bank = psum.tile([P, 2, 2, P], F32, name="turn%d" % b)
-                banks[r, b] = bank
-                for gl in range(2):
-                    for u in range(2):
-                        w0 = 256 * (2 * b + gl)
-                        nc.tensor.transpose(bank[:, u, gl, :], words[:, w0 + u : w0 + 256 : 2], ident[:])
+            bank = psum.tile([P, 2, 2, P], F32, name="turn", bufs=4)
+            banks[r, b] = bank
+            for gl in range(2):
+                for u in range(2):
+                    w0 = 256 * (2 * b + gl)
+                    nc.tensor.transpose(bank[:, u, gl, :], words[:, w0 + u : w0 + 256 : 2], ident[:])
 
         def product(r, b):
-            if b == 0:
-                grouped[r] = flow.tile([P, PASSES, P, 4], BF16, name="grouped", align_bytes=64)
+            if r not in grouped:
+                grouped[r] = flow.tile([P, PASSES, P, 4], BF16, name="grouped", bufs=4, align_bytes=64)
             in0 = banks[r, b][:].bitcast(BF16).rearrange("p u g (i e) -> p g i u e", e=2)
             in1 = scale[:, 2 * b : 2 * b + 2, :].rearrange("p g (u e) -> p g u e", e=2)
             in1 = in1.unsqueeze(2).to_broadcast([P, 2, P, 2, 2])
             dst = grouped[r][:, 2 * b : 2 * b + 2].rearrange("p g i (u e) -> p g i u e", e=2)
             nc.vector.tensor_tensor(out=dst, in0=in0, in1=in1, op=ALU.mult)
 
+        def turned(r, b, engine):
+            if r not in grouped:
+                grouped[r] = flow.tile([P, PASSES, P, 4], BF16, name="grouped", bufs=4, align_bytes=64)
+            dst = grouped[r][:, 2 * b : 2 * b + 2].bitcast(F32)
+            src = banks[r, b][:].rearrange("p u g i -> p g i u")
+            if engine == "v":
+                nc.vector.tensor_copy(out=dst, in_=src)
+            else:
+                nc.scalar.copy(out=dst, in_=src)
+
         def quant_a(r):
-            a_codes[r] = flow.tile([P, PASSES, P], U32, name="acodes", align_bytes=64)
-            a_scales[r] = flow.tile([P, PASSES, P], U8, name="ascales", align_bytes=64)
+            a_codes[r] = flow.tile([P, PASSES, P], U32, name="acodes", bufs=4, align_bytes=64)
+            a_scales[r] = flow.tile([P, PASSES, P], U8, name="ascales", bufs=4, align_bytes=64)
             nc.vector.quantize_mx(
                 out=a_codes[r][:].rearrange("p g i -> p (g i)").bitcast(FP8X4),
                 scales=a_scales[r][:].rearrange("p g i -> p (g i)"),
@@ -122,7 +168,7 @@ def tile_net_pa_w4_kernel(tc, A_bytes, A_scale, features, Wg_words, Wg_scales, b
             )
 
         def first_matmul(r):
-            acc[r] = psum.tile([P, 4, P], F32, name="acc")
+            acc[r] = psum.tile([P, 4, P], F32, name="acc", bufs=1)
             for t in range(4):
                 for g in range(PASSES):
                     nc.tensor.matmul_mx(
@@ -135,13 +181,17 @@ def tile_net_pa_w4_kernel(tc, A_bytes, A_scale, features, Wg_words, Wg_scales, b
                         stop=(g == PASSES - 1),
                     )
 
-        def agg_out(r):
-            g_bf[r] = flow.tile([P, P, 4], BF16, name="gbf", align_bytes=64)
-            nc.scalar.copy(out=g_bf[r][:], in_=acc[r][:].rearrange("p t i -> p i t"))
+        def agg_out(r, engine="s"):
+            g_bf[r] = flow.tile([P, P, 4], BF16, name="gbf", bufs=3, align_bytes=64)
+            src = acc[r][:].rearrange("p t i -> p i t")
+            if engine == "v":
+                nc.vector.tensor_copy(out=g_bf[r][:], in_=src)
+            else:
+                nc.scalar.copy(out=g_bf[r][:], in_=src)
 
         def quant_agg(r):
-            g_codes[r] = flow.tile([P, P], U32, name="gcodes", align_bytes=64)
-            g_scales[r] = flow.tile([P, P], U8, name="gscales", align_bytes=64)
+            g_codes[r] = flow.tile([P, P], U32, name="gcodes", bufs=3, align_bytes=64)
+            g_scales[r] = flow.tile([P, P], U8, name="gscales", bufs=3, align_bytes=64)
             nc.vector.quantize_mx(
                 out=g_codes[r][:].bitcast(FP8X4),
                 scales=g_scales[r][:],
@@ -149,9 +199,9 @@ def tile_net_pa_w4_kernel(tc, A_bytes, A_scale, features, Wg_words, Wg_scales, b
             )
 
         def second_matmul(r):
-            res[r] = psum.tile([P, D], F32, name="res")
+            mid[r] = psum.tile([P, D], F32, name="mid", bufs=2)
             nc.tensor.matmul_mx(
-                out=res[r][:],
+                out=mid[r][:],
                 lhsT=g_codes[r][:].bitcast(FP8X4),
                 lhsT_scale=g_scales[r][:],
                 rhs=w_words[:].bitcast(FP4X4),
@@ -160,35 +210,50 @@ def tile_net_pa_w4_kernel(tc, A_bytes, A_scale, features, Wg_words, Wg_scales, b
                 stop=True,
             )
 
-        raw = {}
-        fin = {}
-        mids = {}
+        def second_matmul_t(r):
+            mid[r] = psum.tile([P, D], F32, name="mid", bufs=2)
+            for c in range(4):
+                nc.tensor.matmul_mx(
+                    out=mid[r][:, c * P : (c + 1) * P],
+                    lhsT=w_words[:, 2 * c * P : 2 * (c + 1) * P].bitcast(FP4X4),
+                    lhsT_scale=w_scales[:, c * P : (c + 1) * P],
+                    rhs=g_codes[r][:].bitcast(FP8X4),
+                    rhs_scale=g_scales[r][:],
+                    start=True,
+                    stop=True,
+                )
 
-        def res_out(r):
-            raw[r] = flow.tile([P, D], F32, name="rawout", align_bytes=64)
-            nc.scalar.copy(out=raw[r][:], in_=res[r][:])
+        def relu_t(r, cs, engine="s"):
+            if r not in t1:
+                t1[r] = flow.tile([P, 4, P], F32, name="t1", bufs=3, align_bytes=64)
+            for c in cs:
+                nc.scalar.activation(
+                    out=t1[r][:, c, :], in_=mid[r][:, c * P : (c + 1) * P], func=ACT.Relu, bias=bias_col[:, c : c + 1]
+                )
 
-        def finish_gp(r):
-            mid = flow.tile([P, D], F32, name="mid", align_bytes=64)
-            fin[r] = flow.tile([P, D], F32, name="fin", align_bytes=64)
-            nc.gpsimd.tensor_tensor(out=mid[:], in0=raw[r][:], in1=bias[:], op=ALU.add)
-            mids[r] = mid
+        def turn_back(r):
+            t2[r] = psum.tile([P, 4, P], F32, name="t2", bufs=1)
+            for c in range(4):
+                nc.tensor.transpose(t2[r][:, c, :], t1[r][:, c, :], ident[:])
 
-        def relu(r):
-            nc.scalar.activation(out=fin[r][:], in_=mids[r][:], func=mybir.ActivationFunctionType.Relu)
-            store(r)
+        def back_out(r, engine="s"):
+            fin = flow.tile([P, D], F32, name="fin", bufs=4, align_bytes=64)
+            src = t2[r][:].rearrange("p c n -> p (c n)")
+            if engine == "v":
+                nc.vector.tensor_copy(out=fin[:], in_=src)
+            else:
+                nc.scalar.copy(out=fin[:], in_=src)
+            nc.sync.dma_start(out=out[r * P : (r + 1) * P, :], in_=fin[:])
 
-        def finish_fast(r):
-            mid = flow.tile([P, D], F32, name="rawout", align_bytes=64)
-            fin[r] = flow.tile([P, D], F32, name="fin", align_bytes=64)
-            for h in range(2):
-                cols = slice(h * 256, (h + 1) * 256)
-                nc.vector.tensor_tensor(out=mid[:, cols], in0=res[r][:, cols], in1=bias[:, cols], op=ALU.add)
-                nc.scalar.activation(out=fin[r][:, cols], in_=mid[:, cols], func=mybir.ActivationFunctionType.Relu)
-            store(r)
-
-        def store(r):
-            nc.sync.dma_start(out=out[r * P : (r + 1) * P, :], in_=fin[r][:])
+        def finish(r, pieces):
+            raw = flow.tile([P, D], F32, name="raw", bufs=4, align_bytes=64)
+            fin = flow.tile([P, D], F32, name="fin", bufs=4, align_bytes=64)
+            w = D // pieces
+            for h in range(pieces):
+                cols = slice(h * w, (h + 1) * w)
+                nc.vector.tensor_tensor(out=raw[:, cols], in0=mid[r][:, cols], in1=bias[:, cols], op=ALU.add)
+                nc.scalar.activation(out=fin[:, cols], in_=raw[:, cols], func=ACT.Relu)
+            nc.sync.dma_start(out=out[r * P : (r + 1) * P, :], in_=fin[:])
 
         def f_interleave(g, engine):
             src = f_raw[g][:].rearrange("p j (m t) -> p t m j", t=4)
@@ -206,54 +271,266 @@ def tile_net_pa_w4_kernel(tc, A_bytes, A_scale, features, Wg_words, Wg_scales, b
                 in_=f_grp[g][:].rearrange("p t m j -> p (t m j)"),
             )
 
-        cast(0, 0, vector=True)
-        cast(0, 1)
+        def bias_column():
+            turned_bias = psum.tile([P, 4, P], BF16, name="turnedbias", tag="t2", bufs=1)
+            for c in range(4):
+                nc.tensor.transpose(turned_bias[:, c, :], bias[:, c * P : (c + 1) * P], ident_bf[:])
+            nc.vector.tensor_copy(out=bias_col[:].rearrange("p (c o) -> p c o", o=1), in_=turned_bias[:, :, 0:1])
+
+        F32_MAX = 3.4028234663852886e38
+        raw = {}
+        summed = {}
+
+        def raw_out(r):
+            raw[r] = flow.tile([P, D], F32, name="raw", bufs=4, align_bytes=64)
+            nc.scalar.copy(out=raw[r][:], in_=mid[r][:])
+
+        def add_g(r, h):
+            if h == 0:
+                summed[r] = flow.tile([P, D], F32, name="summed", bufs=4, align_bytes=64)
+            cols = slice(h * 256, (h + 1) * 256)
+            nc.gpsimd.tensor_tensor(out=summed[r][:, cols], in0=raw[r][:, cols], in1=bias[:, cols], op=ALU.add)
+
+        def add_v(r):
+            summed[r] = flow.tile([P, D], F32, name="summed", bufs=4, align_bytes=64)
+            nc.vector.tensor_tensor(out=summed[r][:], in0=mid[r][:], in1=bias[:], op=ALU.add)
+
+        def relu(r, engine):
+            fin = flow.tile([P, D], F32, name="fin", bufs=4, align_bytes=64)
+            if engine == "g":
+                nc.gpsimd.tensor_scalar(
+                    out=fin[:], in0=summed[r][:], scalar1=F32_MAX, scalar2=0.0, op0=ALU.min, op1=ALU.max
+                )
+            elif engine == "v":
+                nc.vector.tensor_scalar(out=fin[:], in0=summed[r][:], scalar1=0.0, scalar2=None, op0=ALU.max)
+            else:
+                nc.scalar.activation(out=fin[:], in_=summed[r][:], func=ACT.Relu)
+            nc.sync.dma_start(out=out[r * P : (r + 1) * P, :], in_=fin[:])
+
+        LAST = TILES - 1
+        cast(0, 0, "v")
         f_interleave(0, "v")
-        f_interleave(1, "g")
-        turn(0)
-        cast(1, 0)
-        cast(1, 1)
+        cast(0, 1, "s")
+        f_interleave(1, "s")
+        turn(0, 0)
+        turn(0, 1)
+        product(0, 0)
         f_interleave(2, "s")
-        f_interleave(3, "g")
-
-        def within(r, hi=TILES):
-            return 0 <= r < hi
-
-        FAST = TILES - 2
-        for s in range(TILES + 5):
-            if within(s):
-                product(s, 0)
-            if s == 0:
-                f_quant(0)
-            if s == 1:
-                f_quant(2)
-            if within(s + 2):
-                cast(s + 2, 0)
-            if within(s + 1):
-                turn(s + 1)
-            if within(s - 2):
-                agg_out(s - 2)
-            if within(s - 3):
-                second_matmul(s - 3)
-            if within(s - 1):
-                quant_a(s - 1)
-            if within(s):
-                product(s, 1)
-            if s == 0:
-                f_quant(1)
-            if s == 1:
-                f_quant(3)
-            if FAST <= s - 3 < TILES:
-                finish_fast(s - 3)
-            if within(s - 2):
-                quant_agg(s - 2)
-            if within(s - 1):
-                first_matmul(s - 1)
-            if within(s - 3, FAST):
-                res_out(s - 3)
-            if within(s + 2):
-                cast(s + 2, 1)
-            if within(s - 4, FAST):
-                relu(s - 4)
-            if within(s - 3, FAST):
-                finish_gp(s - 3)
+        f_quant(0)
+        product(0, 1)
+        quant_a(0)
+        scaled(1, 0)
+        scaled(1, 1)
+        turn(1, 0)
+        turn(1, 1)
+        f_interleave(3, "s")
+        f_quant(1)
+        scaled(2, 0)
+        turned(1, 1, "s")
+        f_quant(2)
+        scaled(2, 1)
+        f_quant(3)
+        turned(1, 0, "s")
+        turn(2, 0)
+        turn(2, 1)
+        first_matmul(0)
+        quant_a(1)
+        turned(2, 1, "s")
+        agg_out(0, "s")
+        first_matmul(1)
+        turned(2, 0, "s")
+        scaled(3, 0)
+        turn(3, 0)
+        scaled(3, 1)
+        agg_out(1, "s")
+        quant_agg(0)
+        quant_a(2)
+        turned(3, 0, "s")
+        turn(3, 1)
+        scaled(4, 0)
+        scaled(4, 1)
+        first_matmul(2)
+        turned(3, 1, "s")
+        turn(4, 0)
+        turn(4, 1)
+        quant_agg(1)
+        agg_out(2, "s")
+        quant_a(3)
+        second_matmul(0)
+        scaled(5, 0)
+        turned(4, 1, "s")
+        scaled(5, 1)
+        bias_column()
+        second_matmul_t(1)
+        first_matmul(3)
+        turned(4, 0, "s")
+        turn(5, 0)
+        relu_t(1, range(4))
+        turn(5, 1)
+        quant_agg(2)
+        add_v(0)
+        agg_out(3, "s")
+        turn_back(1)
+        quant_a(4)
+        turned(5, 1, "s")
+        second_matmul_t(2)
+        first_matmul(4)
+        turned(5, 0, "s")
+        scaled(6, 0)
+        quant_agg(3)
+        turn(6, 0)
+        relu_t(2, range(4))
+        scaled(6, 1)
+        back_out(1, "s")
+        agg_out(4, "s")
+        turn_back(2)
+        quant_a(5)
+        turned(6, 0, "s")
+        turn(6, 1)
+        scaled(7, 0)
+        scaled(7, 1)
+        first_matmul(5)
+        turned(6, 1, "s")
+        turn(7, 0)
+        turn(7, 1)
+        back_out(2, "s")
+        second_matmul(3)
+        quant_agg(4)
+        agg_out(5, "s")
+        quant_a(6)
+        scaled(8, 0)
+        turned(7, 1, "s")
+        scaled(8, 1)
+        second_matmul_t(4)
+        first_matmul(6)
+        turned(7, 0, "s")
+        turn(8, 0)
+        relu_t(4, range(4))
+        turn(8, 1)
+        add_v(3)
+        quant_agg(5)
+        agg_out(6, "s")
+        turn_back(4)
+        relu(0, "s")
+        quant_a(7)
+        turned(8, 1, "s")
+        second_matmul_t(5)
+        first_matmul(7)
+        turned(8, 0, "s")
+        scaled(9, 0)
+        quant_agg(6)
+        turn(9, 0)
+        relu_t(5, range(4))
+        scaled(9, 1)
+        back_out(4, "s")
+        agg_out(7, "s")
+        turn_back(5)
+        quant_a(8)
+        turned(9, 0, "s")
+        turn(9, 1)
+        scaled(10, 0)
+        scaled(10, 1)
+        first_matmul(8)
+        turned(9, 1, "s")
+        turn(10, 0)
+        turn(10, 1)
+        back_out(5, "s")
+        second_matmul(6)
+        quant_agg(7)
+        agg_out(8, "s")
+        quant_a(9)
+        relu(3, "s")
+        scaled(11, 0)
+        turned(10, 1, "s")
+        scaled(11, 1)
+        second_matmul_t(7)
+        first_matmul(9)
+        turned(10, 0, "s")
+        turn(11, 0)
+        relu_t(7, range(4))
+        turn(11, 1)
+        add_v(6)
+        quant_agg(8)
+        agg_out(9, "s")
+        turn_back(7)
+        quant_a(10)
+        turned(11, 1, "s")
+        second_matmul_t(8)
+        first_matmul(10)
+        turned(11, 0, "s")
+        scaled(12, 0)
+        quant_agg(9)
+        turn(12, 0)
+        relu_t(8, range(4))
+        scaled(12, 1)
+        back_out(7, "s")
+        agg_out(10, "s")
+        turn_back(8)
+        quant_a(11)
+        turned(12, 0, "s")
+        turn(12, 1)
+        scaled(13, 0)
+        scaled(13, 1)
+        first_matmul(11)
+        turned(12, 1, "s")
+        turn(13, 0)
+        turn(13, 1)
+        back_out(8, "s")
+        second_matmul(9)
+        quant_agg(10)
+        agg_out(11, "s")
+        quant_a(12)
+        relu(6, "s")
+        turned(13, 1, "s")
+        second_matmul_t(10)
+        first_matmul(12)
+        turned(13, 0, "s")
+        scaled(14, 0)
+        turn(14, 0)
+        relu_t(10, range(4))
+        scaled(14, 1)
+        add_v(9)
+        quant_agg(11)
+        agg_out(12, "s")
+        turn_back(10)
+        quant_a(13)
+        turned(14, 0, "s")
+        turn(14, 1)
+        second_matmul_t(11)
+        first_matmul(13)
+        turned(14, 1, "s")
+        scaled(15, 0)
+        quant_agg(12)
+        turn(15, 0)
+        relu_t(11, range(4))
+        scaled(15, 1)
+        back_out(10, "s")
+        agg_out(13, "s")
+        turn_back(11)
+        quant_a(14)
+        turned(15, 0, "s")
+        turn(15, 1)
+        turned(15, 1, "s")
+        first_matmul(14)
+        back_out(11, "s")
+        second_matmul(12)
+        quant_agg(13)
+        agg_out(14, "s")
+        quant_a(15)
+        relu(9, "s")
+        second_matmul_t(13)
+        first_matmul(15)
+        quant_agg(14)
+        relu_t(13, range(4))
+        add_v(12)
+        agg_out(15, "s")
+        turn_back(13)
+        quant_agg(15)
+        back_out(13, "s")
+        second_matmul(14)
+        add_v(14)
+        second_matmul(15)
+        relu(12, "s")
+        add_v(15)
+        relu(14, "s")
+        relu(15, "s")

@@ -31,18 +31,18 @@ def tile_net_pa_w4_kernel(tc, A_bytes, A_scale, features, Wg_words, Wg_scales, b
         ctx.enter_context(tc.manual_schedule())
 
         codes_in = [keep.tile([P, NODES], U8, name="abytes%d" % r, align_bytes=64) for r in range(TILES)]
-        scale = keep.tile([P, PASSES, 4], F32, name="scale")
-        spread = [keep.tile([P, NODES // 2], F32, name="spread%d" % h, align_bytes=64) for h in range(2)]
+        vecs = keep.tile([P, PASSES + 1, 4], F32, name="vecs")
+        bias_raw = keep.tile([P, 4], BF16, name="biasraw")
+        spread = keep.tile([P, PASSES + 1, D], F32, name="spread", align_bytes=64)
+        bias = spread[:, PASSES, :]
         f_raw = [keep.tile([P, 4, D], BF16, name="fraw%d" % g, align_bytes=64) for g in range(PASSES)]
         f_grp = [keep.tile([P, 4, P, 4], BF16, name="fgrp%d" % g, align_bytes=64) for g in range(PASSES)]
         f_codes = [keep.tile([P, D], U32, name="fcodes%d" % g, align_bytes=64) for g in range(PASSES)]
         f_scales = [keep.tile([P, D], U8, name="fscales%d" % g, align_bytes=64) for g in range(PASSES)]
         w_words = keep.tile([P, 2 * D], U8, name="wwords", align_bytes=64)
         w_scales = keep.tile([P, D], U8, name="wscales", align_bytes=64)
-        bias = keep.tile([P, D], BF16, name="bias", align_bytes=64)
         bias_col = keep.tile([P, 4], F32, name="biascol")
         ident = keep.tile([P, P], F32, name="ident", align_bytes=64)
-        ident_bf = keep.tile([P, P], BF16, name="identbf", align_bytes=64)
         dummy = keep.tile([P, 1], F32, name="dummy")
         dummy2 = keep.tile([P, 1], F32, name="dummy2")
 
@@ -52,9 +52,28 @@ def tile_net_pa_w4_kernel(tc, A_bytes, A_scale, features, Wg_words, Wg_scales, b
         def load_f(g):
             nc.sync.dma_start(out=f_raw[g][:], in_=features.rearrange("(g p j) c -> g p j c", p=P, j=4)[g])
 
-        def load_spread(h):
-            row = A_scale.rearrange("o k -> (o k)")[h * 1024 : (h + 1) * 1024]
-            nc.sync.dma_start(out=spread[h][:], in_=row.partition_broadcast(P))
+        def load_scale():
+            nc.sync.dma_start(out=vecs[:, 0:PASSES, :], in_=A_scale.rearrange("o (g p t) -> p (o g) t", p=P, t=4))
+
+        def spread_turn(g):
+            bank = psum.tile([P, 4, P], F32, name="spreadbank", tag="turn", bufs=4)
+            banks["s", g] = bank
+            for t in range(4):
+                nc.tensor.transpose(bank[:, t, :], vecs[:, g, t : t + 1].to_broadcast([P, P]), ident[:])
+
+        def spread_out(g, engine):
+            dst = spread[:, g, :].rearrange("p (n t) -> p n t", t=4)
+            src = banks["s", g][:].rearrange("p t n -> p n t")
+            if engine == "v":
+                nc.vector.tensor_copy(out=dst, in_=src)
+            else:
+                nc.scalar.copy(out=dst, in_=src)
+
+        def load_bias():
+            nc.sync.dma_start(out=bias_raw[:], in_=bg.rearrange("(p t) -> p t", t=4))
+
+        def bias_cast():
+            nc.vector.tensor_copy(out=vecs[:, PASSES, :], in_=bias_raw[:])
 
         def load_w():
             nc.sync.dma_start(out=w_words[:], in_=Wg_words.rearrange("g p w -> p (g w)"))
@@ -63,24 +82,19 @@ def tile_net_pa_w4_kernel(tc, A_bytes, A_scale, features, Wg_words, Wg_scales, b
                     out=w_scales[32 * q : 32 * q + 4, :].bitcast(I32),
                     in_=Wg_scales.rearrange("g q n -> (g q) n")[4 * q : 4 * q + 4, :].bitcast(I32),
                 )
-            nc.sync.dma_start(out=bias[:], in_=bg.partition_broadcast(P))
 
         nc.vector.memset(dummy[:], 0.0)
         nc.scalar.copy(out=dummy2[:], in_=dummy[:])
         nc.vector.memset(w_scales[:].bitcast(I32), 0)
         make_identity(nc, ident[:])
-        nc.vector.tensor_copy(out=ident_bf[:], in_=ident[:])
 
-        def load_scale():
-            nc.sync.dma_start(out=scale[:], in_=A_scale.rearrange("o (g p t) -> p (o g) t", p=P, t=4))
-
-        load_a(0)
+        banks = {}
         load_scale()
+        load_bias()
         load_f(0)
+        load_a(0)
         load_f(1)
         load_a(1)
-        load_spread(0)
-        load_spread(1)
         load_f(2)
         load_f(3)
         load_a(2)
@@ -100,7 +114,6 @@ def tile_net_pa_w4_kernel(tc, A_bytes, A_scale, features, Wg_words, Wg_scales, b
         load_a(15)
 
         wide = {}
-        banks = {}
         grouped = {}
         a_codes = {}
         a_scales = {}
@@ -112,41 +125,22 @@ def tile_net_pa_w4_kernel(tc, A_bytes, A_scale, features, Wg_words, Wg_scales, b
         t1 = {}
         t2 = {}
 
-        def cast(r, half, engine):
-            if r not in wide:
-                wide[r] = flow.tile([P, NODES], BF16, name="wide", bufs=5, align_bytes=64)
-            cols = slice(half * 1024, (half + 1) * 1024)
-            src = codes_in[r][:, cols].bitcast(FP8)
-            if engine == "v":
-                nc.vector.tensor_copy(out=wide[r][:, cols], in_=src)
-            else:
-                nc.scalar.copy(out=wide[r][:, cols], in_=src)
-
         def scaled(r, half):
             if r not in wide:
                 wide[r] = flow.tile([P, NODES], BF16, name="wide", bufs=5, align_bytes=64)
             cols = slice(half * 1024, (half + 1) * 1024)
             nc.vector.tensor_tensor(
-                out=wide[r][:, cols], in0=codes_in[r][:, cols].bitcast(FP8), in1=spread[half][:], op=ALU.mult
+                out=wide[r][:, cols], in0=codes_in[r][:, cols].bitcast(FP8), in1=spread[:, 2 * half : 2 * half + 2, :].rearrange("p g k -> p (g k)"), op=ALU.mult
             )
 
         def turn(r, b):
             words = wide[r][:].bitcast(F32)
-            bank = psum.tile([P, 2, 2, P], F32, name="turn", bufs=4)
+            bank = psum.tile([P, 2, 2, P], F32, name="turn", tag="turn", bufs=4)
             banks[r, b] = bank
             for gl in range(2):
                 for u in range(2):
                     w0 = 256 * (2 * b + gl)
                     nc.tensor.transpose(bank[:, u, gl, :], words[:, w0 + u : w0 + 256 : 2], ident[:])
-
-        def product(r, b):
-            if r not in grouped:
-                grouped[r] = flow.tile([P, PASSES, P, 4], BF16, name="grouped", bufs=4, align_bytes=64)
-            in0 = banks[r, b][:].bitcast(BF16).rearrange("p u g (i e) -> p g i u e", e=2)
-            in1 = scale[:, 2 * b : 2 * b + 2, :].rearrange("p g (u e) -> p g u e", e=2)
-            in1 = in1.unsqueeze(2).to_broadcast([P, 2, P, 2, 2])
-            dst = grouped[r][:, 2 * b : 2 * b + 2].rearrange("p g i (u e) -> p g i u e", e=2)
-            nc.vector.tensor_tensor(out=dst, in0=in0, in1=in1, op=ALU.mult)
 
         def turned(r, b, engine):
             if r not in grouped:
@@ -245,15 +239,11 @@ def tile_net_pa_w4_kernel(tc, A_bytes, A_scale, features, Wg_words, Wg_scales, b
                 nc.scalar.copy(out=fin[:], in_=src)
             nc.sync.dma_start(out=out[r * P : (r + 1) * P, :], in_=fin[:])
 
-        def finish(r, pieces):
-            raw = flow.tile([P, D], F32, name="raw", bufs=4, align_bytes=64)
-            fin = flow.tile([P, D], F32, name="fin", bufs=4, align_bytes=64)
-            w = D // pieces
-            for h in range(pieces):
-                cols = slice(h * w, (h + 1) * w)
-                nc.vector.tensor_tensor(out=raw[:, cols], in0=mid[r][:, cols], in1=bias[:, cols], op=ALU.add)
-                nc.scalar.activation(out=fin[:, cols], in_=raw[:, cols], func=ACT.Relu)
-            nc.sync.dma_start(out=out[r * P : (r + 1) * P, :], in_=fin[:])
+        def bias_column():
+            bank = psum.tile([P, 4, P], F32, name="biasbank", tag="t2", bufs=1)
+            for c in range(4):
+                nc.tensor.transpose(bank[:, c, :], bias[:, c * P : (c + 1) * P], ident[:])
+            nc.vector.tensor_copy(out=bias_col[:].rearrange("p (c o) -> p c o", o=1), in_=bank[:, :, 0:1])
 
         def f_interleave(g, engine):
             src = f_raw[g][:].rearrange("p j (m t) -> p t m j", t=4)
@@ -271,266 +261,252 @@ def tile_net_pa_w4_kernel(tc, A_bytes, A_scale, features, Wg_words, Wg_scales, b
                 in_=f_grp[g][:].rearrange("p t m j -> p (t m j)"),
             )
 
-        def bias_column():
-            turned_bias = psum.tile([P, 4, P], BF16, name="turnedbias", tag="t2", bufs=1)
-            for c in range(4):
-                nc.tensor.transpose(turned_bias[:, c, :], bias[:, c * P : (c + 1) * P], ident_bf[:])
-            nc.vector.tensor_copy(out=bias_col[:].rearrange("p (c o) -> p c o", o=1), in_=turned_bias[:, :, 0:1])
-
-        F32_MAX = 3.4028234663852886e38
-        raw = {}
         summed = {}
-
-        def raw_out(r):
-            raw[r] = flow.tile([P, D], F32, name="raw", bufs=4, align_bytes=64)
-            nc.scalar.copy(out=raw[r][:], in_=mid[r][:])
-
-        def add_g(r, h):
-            if h == 0:
-                summed[r] = flow.tile([P, D], F32, name="summed", bufs=4, align_bytes=64)
-            cols = slice(h * 256, (h + 1) * 256)
-            nc.gpsimd.tensor_tensor(out=summed[r][:, cols], in0=raw[r][:, cols], in1=bias[:, cols], op=ALU.add)
 
         def add_v(r):
             summed[r] = flow.tile([P, D], F32, name="summed", bufs=4, align_bytes=64)
-            nc.vector.tensor_tensor(out=summed[r][:], in0=mid[r][:], in1=bias[:], op=ALU.add)
+            nc.vector.tensor_tensor(out=summed[r][:], in0=mid[r][:], in1=bias, op=ALU.add)
 
         def relu(r, engine):
             fin = flow.tile([P, D], F32, name="fin", bufs=4, align_bytes=64)
-            if engine == "g":
-                nc.gpsimd.tensor_scalar(
-                    out=fin[:], in0=summed[r][:], scalar1=F32_MAX, scalar2=0.0, op0=ALU.min, op1=ALU.max
-                )
-            elif engine == "v":
+            if engine == "v":
                 nc.vector.tensor_scalar(out=fin[:], in0=summed[r][:], scalar1=0.0, scalar2=None, op0=ALU.max)
             else:
                 nc.scalar.activation(out=fin[:], in_=summed[r][:], func=ACT.Relu)
             nc.sync.dma_start(out=out[r * P : (r + 1) * P, :], in_=fin[:])
 
-        LAST = TILES - 1
-        cast(0, 0, "v")
+        bias_cast()
+        spread_turn(1)
+        spread_turn(0)
+        spread_out(1, "s")
+        spread_turn(3)
+        spread_out(0, "s")
         f_interleave(0, "v")
-        cast(0, 1, "s")
+        spread_turn(2)
+        spread_out(3, "s")
         f_interleave(1, "s")
-        turn(0, 0)
-        turn(0, 1)
-        product(0, 0)
-        f_interleave(2, "s")
         f_quant(0)
-        product(0, 1)
-        quant_a(0)
-        scaled(1, 0)
-        scaled(1, 1)
-        turn(1, 0)
-        turn(1, 1)
+        spread_out(2, "s")
+        spread_turn(4)
+        spread_out(4, "s")
         f_interleave(3, "s")
-        f_quant(1)
-        scaled(2, 0)
-        turned(1, 1, "s")
-        f_quant(2)
-        scaled(2, 1)
-        f_quant(3)
-        turned(1, 0, "s")
-        turn(2, 0)
-        turn(2, 1)
-        first_matmul(0)
-        quant_a(1)
-        turned(2, 1, "s")
-        agg_out(0, "s")
-        first_matmul(1)
-        turned(2, 0, "s")
+        scaled(1, 0)
+        f_interleave(2, "s")
+        scaled(0, 0)
+        scaled(0, 1)
+        turn(0, 0)
         scaled(3, 0)
+        turned(0, 0, "s")
+        turn(0, 1)
+        turned(0, 1, "s")
+        turn(1, 0)
+        scaled(1, 1)
+        scaled(2, 0)
+        f_quant(3)
+        f_quant(1)
+        f_quant(2)
+        quant_a(0)
+        turn(1, 1)
+        scaled(2, 1)
+        turn(2, 0)
+        first_matmul(0)
+        scaled(5, 0)
+        turned(1, 0, "s")
+        turned(1, 1, "s")
+        turned(2, 0, "s")
+        agg_out(0, "s")
+        quant_a(1)
+        turn(2, 1)
+        turned(2, 1, "s")
         turn(3, 0)
+        first_matmul(1)
         scaled(3, 1)
-        agg_out(1, "s")
-        quant_agg(0)
-        quant_a(2)
-        turned(3, 0, "s")
-        turn(3, 1)
         scaled(4, 0)
+        agg_out(1, "s")
+        quant_a(2)
+        turn(3, 1)
         scaled(4, 1)
-        first_matmul(2)
-        turned(3, 1, "s")
         turn(4, 0)
-        turn(4, 1)
         quant_agg(1)
+        first_matmul(2)
+        scaled(7, 0)
+        turned(3, 0, "s")
+        quant_agg(0)
+        turned(3, 1, "s")
+        turned(4, 0, "s")
         agg_out(2, "s")
         quant_a(3)
-        second_matmul(0)
-        scaled(5, 0)
+        turn(4, 1)
         turned(4, 1, "s")
-        scaled(5, 1)
+        turn(5, 0)
         bias_column()
         second_matmul_t(1)
+        second_matmul(0)
         first_matmul(3)
-        turned(4, 0, "s")
-        turn(5, 0)
-        relu_t(1, range(4))
-        turn(5, 1)
-        quant_agg(2)
-        add_v(0)
-        agg_out(3, "s")
-        turn_back(1)
-        quant_a(4)
-        turned(5, 1, "s")
-        second_matmul_t(2)
-        first_matmul(4)
-        turned(5, 0, "s")
+        scaled(5, 1)
         scaled(6, 0)
-        quant_agg(3)
-        turn(6, 0)
-        relu_t(2, range(4))
+        relu_t(1, range(4))
+        turn_back(1)
+        agg_out(3, "s")
+        quant_a(4)
+        turn(5, 1)
         scaled(6, 1)
+        turn(6, 0)
+        quant_agg(3)
+        first_matmul(4)
+        scaled(9, 0)
+        turned(5, 0, "s")
+        add_v(0)
+        quant_agg(2)
+        turned(5, 1, "s")
         back_out(1, "s")
-        agg_out(4, "s")
-        turn_back(2)
-        quant_a(5)
         turned(6, 0, "s")
+        agg_out(4, "s")
+        relu(0, "s")
+        quant_a(5)
         turn(6, 1)
-        scaled(7, 0)
-        scaled(7, 1)
-        first_matmul(5)
         turned(6, 1, "s")
         turn(7, 0)
-        turn(7, 1)
-        back_out(2, "s")
-        second_matmul(3)
-        quant_agg(4)
+        second_matmul_t(3)
+        second_matmul(2)
+        first_matmul(5)
+        scaled(7, 1)
+        scaled(8, 0)
+        relu_t(3, range(4))
+        turn_back(3)
         agg_out(5, "s")
         quant_a(6)
-        scaled(8, 0)
-        turned(7, 1, "s")
+        turn(7, 1)
         scaled(8, 1)
-        second_matmul_t(4)
-        first_matmul(6)
-        turned(7, 0, "s")
         turn(8, 0)
-        relu_t(4, range(4))
-        turn(8, 1)
-        add_v(3)
         quant_agg(5)
-        agg_out(6, "s")
-        turn_back(4)
-        relu(0, "s")
-        quant_a(7)
-        turned(8, 1, "s")
-        second_matmul_t(5)
-        first_matmul(7)
-        turned(8, 0, "s")
-        scaled(9, 0)
-        quant_agg(6)
-        turn(9, 0)
-        relu_t(5, range(4))
-        scaled(9, 1)
-        back_out(4, "s")
-        agg_out(7, "s")
-        turn_back(5)
-        quant_a(8)
-        turned(9, 0, "s")
-        turn(9, 1)
-        scaled(10, 0)
-        scaled(10, 1)
-        first_matmul(8)
-        turned(9, 1, "s")
-        turn(10, 0)
-        turn(10, 1)
-        back_out(5, "s")
-        second_matmul(6)
-        quant_agg(7)
-        agg_out(8, "s")
-        quant_a(9)
-        relu(3, "s")
+        first_matmul(6)
         scaled(11, 0)
-        turned(10, 1, "s")
-        scaled(11, 1)
-        second_matmul_t(7)
-        first_matmul(9)
+        turned(7, 0, "s")
+        add_v(2)
+        quant_agg(4)
+        turned(7, 1, "s")
+        back_out(3, "s")
+        turned(8, 0, "s")
+        agg_out(6, "s")
+        relu(2, "s")
+        quant_a(7)
+        turn(8, 1)
+        turned(8, 1, "s")
+        turn(9, 0)
+        second_matmul_t(5)
+        second_matmul(4)
+        first_matmul(7)
+        scaled(9, 1)
+        scaled(10, 0)
+        relu_t(5, range(4))
+        turn_back(5)
+        agg_out(7, "s")
+        quant_a(8)
+        turn(9, 1)
+        scaled(10, 1)
+        turn(10, 0)
+        quant_agg(7)
+        first_matmul(8)
+        scaled(13, 0)
+        turned(9, 0, "s")
+        add_v(4)
+        quant_agg(6)
+        turned(9, 1, "s")
+        back_out(5, "s")
         turned(10, 0, "s")
+        agg_out(8, "s")
+        relu(4, "s")
+        quant_a(9)
+        turn(10, 1)
+        turned(10, 1, "s")
         turn(11, 0)
+        second_matmul_t(7)
+        second_matmul(6)
+        first_matmul(9)
+        scaled(11, 1)
+        scaled(12, 0)
         relu_t(7, range(4))
-        turn(11, 1)
-        add_v(6)
-        quant_agg(8)
-        agg_out(9, "s")
         turn_back(7)
+        agg_out(9, "s")
         quant_a(10)
-        turned(11, 1, "s")
-        second_matmul_t(8)
+        turn(11, 1)
+        scaled(12, 1)
+        turn(12, 0)
+        quant_agg(9)
         first_matmul(10)
         turned(11, 0, "s")
-        scaled(12, 0)
-        quant_agg(9)
-        turn(12, 0)
-        relu_t(8, range(4))
-        scaled(12, 1)
+        add_v(6)
+        quant_agg(8)
+        turned(11, 1, "s")
         back_out(7, "s")
-        agg_out(10, "s")
-        turn_back(8)
-        quant_a(11)
         turned(12, 0, "s")
+        agg_out(10, "s")
+        relu(6, "s")
+        quant_a(11)
         turn(12, 1)
-        scaled(13, 0)
-        scaled(13, 1)
-        first_matmul(11)
         turned(12, 1, "s")
         turn(13, 0)
-        turn(13, 1)
-        back_out(8, "s")
-        second_matmul(9)
-        quant_agg(10)
+        second_matmul_t(9)
+        second_matmul(8)
+        first_matmul(11)
+        scaled(13, 1)
+        scaled(14, 0)
+        relu_t(9, range(4))
+        turn_back(9)
         agg_out(11, "s")
         quant_a(12)
-        relu(6, "s")
-        turned(13, 1, "s")
-        second_matmul_t(10)
+        turn(13, 1)
+        scaled(14, 1)
+        turn(14, 0)
+        quant_agg(11)
         first_matmul(12)
         turned(13, 0, "s")
-        scaled(14, 0)
-        turn(14, 0)
-        relu_t(10, range(4))
-        scaled(14, 1)
-        add_v(9)
-        quant_agg(11)
-        agg_out(12, "s")
-        turn_back(10)
-        quant_a(13)
-        turned(14, 0, "s")
-        turn(14, 1)
-        second_matmul_t(11)
-        first_matmul(13)
-        turned(14, 1, "s")
         scaled(15, 0)
-        quant_agg(12)
-        turn(15, 0)
-        relu_t(11, range(4))
+        add_v(8)
+        quant_agg(10)
+        turned(13, 1, "s")
+        back_out(9, "s")
+        turned(14, 0, "s")
+        agg_out(12, "s")
+        relu(8, "s")
+        quant_a(13)
+        turn(14, 1)
         scaled(15, 1)
-        back_out(10, "s")
-        agg_out(13, "s")
-        turn_back(11)
-        quant_a(14)
+        turn(15, 0)
+        turned(14, 1, "s")
+        second_matmul_t(11)
+        second_matmul(10)
+        first_matmul(13)
+        relu_t(11, range(4))
         turned(15, 0, "s")
+        turn_back(11)
+        agg_out(13, "s")
         turn(15, 1)
+        quant_a(14)
         turned(15, 1, "s")
-        first_matmul(14)
-        back_out(11, "s")
-        second_matmul(12)
         quant_agg(13)
+        first_matmul(14)
+        add_v(10)
+        quant_agg(12)
+        back_out(11, "s")
         agg_out(14, "s")
+        relu(10, "s")
         quant_a(15)
-        relu(9, "s")
         second_matmul_t(13)
+        second_matmul(12)
         first_matmul(15)
-        quant_agg(14)
         relu_t(13, range(4))
-        add_v(12)
-        agg_out(15, "s")
         turn_back(13)
-        quant_agg(15)
+        agg_out(15, "s")
+        add_v(12)
+        quant_agg(14)
         back_out(13, "s")
-        second_matmul(14)
-        add_v(14)
-        second_matmul(15)
         relu(12, "s")
-        add_v(15)
+        second_matmul(14)
+        quant_agg(15)
+        second_matmul(15)
+        add_v(14)
         relu(14, "s")
+        add_v(15)
         relu(15, "s")

from contextlib import ExitStack

import concourse.mybir as mybir
from concourse.masks import make_identity

F32 = mybir.dt.float32
BF16 = mybir.dt.bfloat16
U32 = mybir.dt.uint32
I32 = mybir.dt.int32
U8 = mybir.dt.uint8
FP8 = mybir.dt.float8_e4m3fn
FP8X4 = mybir.dt.float8_e4m3fn_x4
FP4X4 = mybir.dt.float4_e2m1fn_x4
ALU = mybir.AluOpType
ACT = mybir.ActivationFunctionType

NODES = 2048
D = 512
P = 128
PASSES = NODES // 512
TILES = NODES // P
FLOPS = 2 * NODES * NODES * D + 2 * NODES * D * D


def tile_net_pa_w4_kernel(tc, A_bytes, A_scale, features, Wg_words, Wg_scales, bg, out):
    nc = tc.nc
    with ExitStack() as ctx:
        keep = ctx.enter_context(tc.tile_pool(name="keep", bufs=1))
        flow = ctx.enter_context(tc.tile_pool(name="flow", bufs=3))
        psum = ctx.enter_context(tc.psum_pool(name="psum", bufs=1))
        ctx.enter_context(tc.manual_schedule())

        codes_in = [keep.tile([P, NODES], U8, name="abytes%d" % r, align_bytes=64) for r in range(TILES)]
        vecs = keep.tile([P, PASSES + 1, 4], F32, name="vecs")
        bias_raw = keep.tile([P, 4], BF16, name="biasraw")
        spread = keep.tile([P, PASSES + 1, D], F32, name="spread", align_bytes=64)
        bias = spread[:, PASSES, :]
        f_raw = [keep.tile([P, 4, D], BF16, name="fraw%d" % g, align_bytes=64) for g in range(PASSES)]
        f_grp = [keep.tile([P, 4, P, 4], BF16, name="fgrp%d" % g, align_bytes=64) for g in range(PASSES)]
        f_codes = [keep.tile([P, D], U32, name="fcodes%d" % g, align_bytes=64) for g in range(PASSES)]
        f_scales = [keep.tile([P, D], U8, name="fscales%d" % g, align_bytes=64) for g in range(PASSES)]
        w_words = keep.tile([P, 2 * D], U8, name="wwords", align_bytes=64)
        w_scales = keep.tile([P, D], U8, name="wscales", align_bytes=64)
        bias_col = keep.tile([P, 4], F32, name="biascol")
        ident = keep.tile([P, P], F32, name="ident", align_bytes=64)
        dummy = keep.tile([P, 1], F32, name="dummy")
        dummy2 = keep.tile([P, 1], F32, name="dummy2")

        def load_a(r):
            nc.sync.dma_start(out=codes_in[r][:], in_=A_bytes[r * P : (r + 1) * P, :])

        def load_f(g):
            nc.sync.dma_start(out=f_raw[g][:], in_=features.rearrange("(g p j) c -> g p j c", p=P, j=4)[g])

        def load_scale():
            nc.sync.dma_start(out=vecs[:, 0:PASSES, :], in_=A_scale.rearrange("o (g p t) -> p (o g) t", p=P, t=4))

        def spread_turn(g):
            bank = psum.tile([P, 4, P], F32, name="spreadbank", tag="turn", bufs=4)
            banks["s", g] = bank
            for t in range(4):
                nc.tensor.transpose(bank[:, t, :], vecs[:, g, t : t + 1].to_broadcast([P, P]), ident[:])

        def spread_out(g, engine):
            dst = spread[:, g, :].rearrange("p (n t) -> p n t", t=4)
            src = banks["s", g][:].rearrange("p t n -> p n t")
            if engine == "v":
                nc.vector.tensor_copy(out=dst, in_=src)
            else:
                nc.scalar.copy(out=dst, in_=src)

        def load_bias():
            nc.sync.dma_start(out=bias_raw[:], in_=bg.rearrange("(p t) -> p t", t=4))

        def bias_cast():
            nc.vector.tensor_copy(out=vecs[:, PASSES, :], in_=bias_raw[:])

        def load_w():
            nc.sync.dma_start(out=w_words[:], in_=Wg_words.rearrange("g p w -> p (g w)"))
            for q in range(4):
                nc.sync.dma_start(
                    out=w_scales[32 * q : 32 * q + 4, :].bitcast(I32),
                    in_=Wg_scales.rearrange("g q n -> (g q) n")[4 * q : 4 * q + 4, :].bitcast(I32),
                )

        nc.vector.memset(dummy[:], 0.0)
        nc.scalar.copy(out=dummy2[:], in_=dummy[:])
        nc.vector.memset(w_scales[:].bitcast(I32), 0)
        make_identity(nc, ident[:])

        banks = {}
        load_scale()
        load_bias()
        load_f(0)
        load_a(0)
        load_f(1)
        load_a(1)
        load_f(2)
        load_f(3)
        load_a(2)
        load_w()
        load_a(3)
        load_a(4)
        load_a(5)
        load_a(6)
        load_a(7)
        load_a(8)
        load_a(9)
        load_a(10)
        load_a(11)
        load_a(12)
        load_a(13)
        load_a(14)
        load_a(15)

        wide = {}
        grouped = {}
        a_codes = {}
        a_scales = {}
        acc = {}
        g_bf = {}
        g_codes = {}
        g_scales = {}
        mid = {}
        t1 = {}
        t2 = {}

        def scaled(r, half):
            if r not in wide:
                wide[r] = flow.tile([P, NODES], BF16, name="wide", bufs=5, align_bytes=64)
            cols = slice(half * 1024, (half + 1) * 1024)
            nc.vector.tensor_tensor(
                out=wide[r][:, cols], in0=codes_in[r][:, cols].bitcast(FP8), in1=spread[:, 2 * half : 2 * half + 2, :].rearrange("p g k -> p (g k)"), op=ALU.mult
            )

        def turn(r, b):
            words = wide[r][:].bitcast(F32)
            bank = psum.tile([P, 2, 2, P], F32, name="turn", tag="turn", bufs=4)
            banks[r, b] = bank
            for gl in range(2):
                for u in range(2):
                    w0 = 256 * (2 * b + gl)
                    nc.tensor.transpose(bank[:, u, gl, :], words[:, w0 + u : w0 + 256 : 2], ident[:])

        def turned(r, b, engine):
            if r not in grouped:
                grouped[r] = flow.tile([P, PASSES, P, 4], BF16, name="grouped", bufs=4, align_bytes=64)
            dst = grouped[r][:, 2 * b : 2 * b + 2].bitcast(F32)
            src = banks[r, b][:].rearrange("p u g i -> p g i u")
            if engine == "v":
                nc.vector.tensor_copy(out=dst, in_=src)
            else:
                nc.scalar.copy(out=dst, in_=src)

        def quant_a(r):
            a_codes[r] = flow.tile([P, PASSES, P], U32, name="acodes", bufs=4, align_bytes=64)
            a_scales[r] = flow.tile([P, PASSES, P], U8, name="ascales", bufs=4, align_bytes=64)
            nc.vector.quantize_mx(
                out=a_codes[r][:].rearrange("p g i -> p (g i)").bitcast(FP8X4),
                scales=a_scales[r][:].rearrange("p g i -> p (g i)"),
                in_=grouped[r][:].rearrange("p g i t -> p (g i t)"),
            )

        def first_matmul(r):
            acc[r] = psum.tile([P, 4, P], F32, name="acc", bufs=1)
            for t in range(4):
                for g in range(PASSES):
                    nc.tensor.matmul_mx(
                        out=acc[r][:, t, :],
                        lhsT=f_codes[g][:, t * P : (t + 1) * P].bitcast(FP8X4),
                        lhsT_scale=f_scales[g][:, t * P : (t + 1) * P],
                        rhs=a_codes[r][:, g, :].bitcast(FP8X4),
                        rhs_scale=a_scales[r][:, g, :],
                        start=(g == 0),
                        stop=(g == PASSES - 1),
                    )

        def agg_out(r, engine="s"):
            g_bf[r] = flow.tile([P, P, 4], BF16, name="gbf", bufs=3, align_bytes=64)
            src = acc[r][:].rearrange("p t i -> p i t")
            if engine == "v":
                nc.vector.tensor_copy(out=g_bf[r][:], in_=src)
            else:
                nc.scalar.copy(out=g_bf[r][:], in_=src)

        def quant_agg(r):
            g_codes[r] = flow.tile([P, P], U32, name="gcodes", bufs=3, align_bytes=64)
            g_scales[r] = flow.tile([P, P], U8, name="gscales", bufs=3, align_bytes=64)
            nc.vector.quantize_mx(
                out=g_codes[r][:].bitcast(FP8X4),
                scales=g_scales[r][:],
                in_=g_bf[r][:].rearrange("p i t -> p (i t)"),
            )

        def second_matmul(r):
            mid[r] = psum.tile([P, D], F32, name="mid", bufs=2)
            nc.tensor.matmul_mx(
                out=mid[r][:],
                lhsT=g_codes[r][:].bitcast(FP8X4),
                lhsT_scale=g_scales[r][:],
                rhs=w_words[:].bitcast(FP4X4),
                rhs_scale=w_scales[:],
                start=True,
                stop=True,
            )

        def second_matmul_t(r):
            mid[r] = psum.tile([P, D], F32, name="mid", bufs=2)
            for c in range(4):
                nc.tensor.matmul_mx(
                    out=mid[r][:, c * P : (c + 1) * P],
                    lhsT=w_words[:, 2 * c * P : 2 * (c + 1) * P].bitcast(FP4X4),
                    lhsT_scale=w_scales[:, c * P : (c + 1) * P],
                    rhs=g_codes[r][:].bitcast(FP8X4),
                    rhs_scale=g_scales[r][:],
                    start=True,
                    stop=True,
                )

        def relu_t(r, cs, engine="s"):
            if r not in t1:
                t1[r] = flow.tile([P, 4, P], F32, name="t1", bufs=3, align_bytes=64)
            for c in cs:
                nc.scalar.activation(
                    out=t1[r][:, c, :], in_=mid[r][:, c * P : (c + 1) * P], func=ACT.Relu, bias=bias_col[:, c : c + 1]
                )

        def turn_back(r):
            t2[r] = psum.tile([P, 4, P], F32, name="t2", bufs=1)
            for c in range(4):
                nc.tensor.transpose(t2[r][:, c, :], t1[r][:, c, :], ident[:])

        def back_out(r, engine="s"):
            fin = flow.tile([P, D], F32, name="fin", bufs=4, align_bytes=64)
            src = t2[r][:].rearrange("p c n -> p (c n)")
            if engine == "v":
                nc.vector.tensor_copy(out=fin[:], in_=src)
            else:
                nc.scalar.copy(out=fin[:], in_=src)
            nc.sync.dma_start(out=out[r * P : (r + 1) * P, :], in_=fin[:])

        def bias_column():
            bank = psum.tile([P, 4, P], F32, name="biasbank", tag="t2", bufs=1)
            for c in range(4):
                nc.tensor.transpose(bank[:, c, :], bias[:, c * P : (c + 1) * P], ident[:])
            nc.vector.tensor_copy(out=bias_col[:].rearrange("p (c o) -> p c o", o=1), in_=bank[:, :, 0:1])

        def f_interleave(g, engine):
            src = f_raw[g][:].rearrange("p j (m t) -> p t m j", t=4)
            if engine == "v":
                nc.vector.tensor_copy(out=f_grp[g][:], in_=src)
            elif engine == "s":
                nc.scalar.copy(out=f_grp[g][:], in_=src)
            else:
                nc.gpsimd.tensor_scalar(out=f_grp[g][:], in0=src, scalar1=1.0, scalar2=0.0, op0=ALU.mult, op1=ALU.add)

        def f_quant(g):
            nc.vector.quantize_mx(
                out=f_codes[g][:].bitcast(FP8X4),
                scales=f_scales[g][:],
                in_=f_grp[g][:].rearrange("p t m j -> p (t m j)"),
            )

        summed = {}

        def add_v(r):
            summed[r] = flow.tile([P, D], F32, name="summed", bufs=4, align_bytes=64)
            nc.vector.tensor_tensor(out=summed[r][:], in0=mid[r][:], in1=bias, op=ALU.add)

        def relu(r, engine):
            fin = flow.tile([P, D], F32, name="fin", bufs=4, align_bytes=64)
            if engine == "v":
                nc.vector.tensor_scalar(out=fin[:], in0=summed[r][:], scalar1=0.0, scalar2=None, op0=ALU.max)
            else:
                nc.scalar.activation(out=fin[:], in_=summed[r][:], func=ACT.Relu)
            nc.sync.dma_start(out=out[r * P : (r + 1) * P, :], in_=fin[:])

        bias_cast()
        spread_turn(1)
        spread_turn(0)
        spread_out(1, "s")
        spread_turn(3)
        spread_out(0, "s")
        f_interleave(0, "v")
        spread_turn(2)
        spread_out(3, "s")
        f_interleave(1, "s")
        f_quant(0)
        spread_out(2, "s")
        spread_turn(4)
        spread_out(4, "s")
        f_interleave(3, "s")
        scaled(1, 0)
        f_interleave(2, "s")
        scaled(0, 0)
        scaled(0, 1)
        turn(0, 0)
        scaled(3, 0)
        turned(0, 0, "s")
        turn(0, 1)
        turned(0, 1, "s")
        turn(1, 0)
        scaled(1, 1)
        scaled(2, 0)
        f_quant(3)
        f_quant(1)
        f_quant(2)
        quant_a(0)
        turn(1, 1)
        scaled(2, 1)
        turn(2, 0)
        first_matmul(0)
        scaled(5, 0)
        turned(1, 0, "s")
        turned(1, 1, "s")
        turned(2, 0, "s")
        agg_out(0, "s")
        quant_a(1)
        turn(2, 1)
        turned(2, 1, "s")
        turn(3, 0)
        first_matmul(1)
        scaled(3, 1)
        scaled(4, 0)
        agg_out(1, "s")
        quant_a(2)
        turn(3, 1)
        scaled(4, 1)
        turn(4, 0)
        quant_agg(1)
        first_matmul(2)
        scaled(7, 0)
        turned(3, 0, "s")
        quant_agg(0)
        turned(3, 1, "s")
        turned(4, 0, "s")
        agg_out(2, "s")
        quant_a(3)
        turn(4, 1)
        turned(4, 1, "s")
        turn(5, 0)
        bias_column()
        second_matmul_t(1)
        second_matmul(0)
        first_matmul(3)
        scaled(5, 1)
        scaled(6, 0)
        relu_t(1, range(4))
        turn_back(1)
        agg_out(3, "s")
        quant_a(4)
        turn(5, 1)
        scaled(6, 1)
        turn(6, 0)
        quant_agg(3)
        first_matmul(4)
        scaled(9, 0)
        turned(5, 0, "s")
        add_v(0)
        quant_agg(2)
        turned(5, 1, "s")
        back_out(1, "s")
        turned(6, 0, "s")
        agg_out(4, "s")
        relu(0, "s")
        quant_a(5)
        turn(6, 1)
        turned(6, 1, "s")
        turn(7, 0)
        second_matmul_t(3)
        second_matmul(2)
        first_matmul(5)
        scaled(7, 1)
        scaled(8, 0)
        relu_t(3, range(4))
        turn_back(3)
        agg_out(5, "s")
        quant_a(6)
        turn(7, 1)
        scaled(8, 1)
        turn(8, 0)
        quant_agg(5)
        first_matmul(6)
        scaled(11, 0)
        turned(7, 0, "s")
        add_v(2)
        quant_agg(4)
        turned(7, 1, "s")
        back_out(3, "s")
        turned(8, 0, "s")
        agg_out(6, "s")
        relu(2, "s")
        quant_a(7)
        turn(8, 1)
        turned(8, 1, "s")
        turn(9, 0)
        second_matmul_t(5)
        second_matmul(4)
        first_matmul(7)
        scaled(9, 1)
        scaled(10, 0)
        relu_t(5, range(4))
        turn_back(5)
        agg_out(7, "s")
        quant_a(8)
        turn(9, 1)
        scaled(10, 1)
        turn(10, 0)
        quant_agg(7)
        first_matmul(8)
        scaled(13, 0)
        turned(9, 0, "s")
        add_v(4)
        quant_agg(6)
        turned(9, 1, "s")
        back_out(5, "s")
        turned(10, 0, "s")
        agg_out(8, "s")
        relu(4, "s")
        quant_a(9)
        turn(10, 1)
        turned(10, 1, "s")
        turn(11, 0)
        second_matmul_t(7)
        second_matmul(6)
        first_matmul(9)
        scaled(11, 1)
        scaled(12, 0)
        relu_t(7, range(4))
        turn_back(7)
        agg_out(9, "s")
        quant_a(10)
        turn(11, 1)
        scaled(12, 1)
        turn(12, 0)
        quant_agg(9)
        first_matmul(10)
        turned(11, 0, "s")
        add_v(6)
        quant_agg(8)
        turned(11, 1, "s")
        back_out(7, "s")
        turned(12, 0, "s")
        agg_out(10, "s")
        relu(6, "s")
        quant_a(11)
        turn(12, 1)
        turned(12, 1, "s")
        turn(13, 0)
        second_matmul_t(9)
        second_matmul(8)
        first_matmul(11)
        scaled(13, 1)
        scaled(14, 0)
        relu_t(9, range(4))
        turn_back(9)
        agg_out(11, "s")
        quant_a(12)
        turn(13, 1)
        scaled(14, 1)
        turn(14, 0)
        quant_agg(11)
        first_matmul(12)
        turned(13, 0, "s")
        scaled(15, 0)
        add_v(8)
        quant_agg(10)
        turned(13, 1, "s")
        back_out(9, "s")
        turned(14, 0, "s")
        agg_out(12, "s")
        relu(8, "s")
        quant_a(13)
        turn(14, 1)
        scaled(15, 1)
        turn(15, 0)
        turned(14, 1, "s")
        second_matmul_t(11)
        second_matmul(10)
        first_matmul(13)
        relu_t(11, range(4))
        turned(15, 0, "s")
        turn_back(11)
        agg_out(13, "s")
        turn(15, 1)
        quant_a(14)
        turned(15, 1, "s")
        quant_agg(13)
        first_matmul(14)
        add_v(10)
        quant_agg(12)
        back_out(11, "s")
        agg_out(14, "s")
        relu(10, "s")
        quant_a(15)
        second_matmul_t(13)
        second_matmul(12)
        first_matmul(15)
        relu_t(13, range(4))
        turn_back(13)
        agg_out(15, "s")
        add_v(12)
        quant_agg(14)
        back_out(13, "s")
        relu(12, "s")
        second_matmul(14)
        quant_agg(15)
        second_matmul(15)
        add_v(14)
        relu(14, "s")
        add_v(15)
        relu(15, "s")
